import numpy as np
import ml_dtypes


def mxq(x, axis, fmt="e4m3"):
    dtype, down = {"e4m3": (ml_dtypes.float8_e4m3fn, 7), "e5m2": (ml_dtypes.float8_e5m2, 14)}[fmt]
    v = np.moveaxis(np.asarray(x, np.float32).astype(ml_dtypes.bfloat16).astype(np.float64), axis, -1)
    blocks = v.reshape(v.shape[:-1] + (-1, 32))
    amax = np.abs(blocks).max(-1, keepdims=True)
    byte = np.maximum(np.where(amax > 0, np.frexp(amax)[1] - 1 + 127, 0) - down, 1)
    scale = np.exp2(byte - 127.0)
    codes = (blocks / scale).astype(np.float32).astype(dtype).astype(np.float64)
    return np.moveaxis((codes * scale).reshape(v.shape), -1, axis)


WIDE = False


def mx_kscale(k):
    if not WIDE:
        return np.ones(k)
    levels = np.array([10, -10, 5, -5, 0])
    if k % 512:
        return np.exp2(np.random.permutation(np.resize(levels, k // 32))).repeat(32)
    a = np.empty((k // 512, 16))
    for p in range(k // 512):
        a[p, :8] = np.random.permutation(np.resize(levels, 8))
        for g in range(8):
            far = levels[np.abs(levels - a[p, g]) >= 10]
            a[p, g + 8] = far[np.random.randint(len(far))]
    return np.exp2(a.ravel()).repeat(32)


BF16 = ml_dtypes.bfloat16


def bf(x):
    return np.asarray(x, np.float32).astype(BF16)


def f64(x):
    return np.asarray(x).astype(np.float64)


B, L, D = 3, 512, 512
SIG = 2.0


def setup_inputs():
    s, t = mx_kscale(D), mx_kscale(D)
    return {"x1": bf(np.random.standard_normal((B, L, D)) * s),
            "bi_linear_w": bf(np.random.standard_normal((D, D)) * SIG / D / s[:, None] * t),
            "x2": bf(np.random.standard_normal((B, L, D)) / t)}


def reference(x1, bi_linear_w, x2):
    h = mxq(f64(x1), 2, "e4m3") @ mxq(f64(bi_linear_w), 0, "e4m3")
    return mxq(h, 2, "e4m3") @ mxq(f64(x2), 2, "e4m3").transpose(0, 2, 1)

@@ -1,0 +1,200 @@
+from contextlib import ExitStack
+
+import concourse.mybir as mybir
+from concourse.masks import make_identity
+
+F32 = mybir.dt.float32
+BF16 = mybir.dt.bfloat16
+U32 = mybir.dt.uint32
+U8 = mybir.dt.uint8
+FP8X4 = mybir.dt.float8_e4m3fn_x4
+
+P = 128
+PACK = 4
+B, L, D = 3, 512, 512
+BANK = 512
+N_BANKS = 8
+FLOPS = 2 * 2 * B * L * D * D
+
+
+def tile_coattentionandcombine_pa_kernel(tc, x1, bi_linear_w, x2, out):
+    nc = tc.nc
+    with ExitStack() as ctx:
+        sbuf = ctx.enter_context(tc.tile_pool(name="sbuf", bufs=1))
+        psum = ctx.enter_context(tc.psum_pool(name="psum", bufs=N_BANKS))
+        ctx.enter_context(tc.manual_schedule())
+
+        def quantisable(name, columns):
+            return (
+                sbuf.tile([P, columns * PACK], BF16, name=name + "_grouped", align_bytes=64),
+                sbuf.tile([P, columns], U32, name=name + "_words", align_bytes=64),
+                sbuf.tile([P, columns], U8, name=name + "_scales", align_bytes=64),
+            )
+
+        def quantise(operand, first, last):
+            grouped, words, scales = operand
+            nc.vector.quantize_mx(
+                out=words[:, first:last].bitcast(FP8X4),
+                scales=scales[:, first:last],
+                in_=grouped[:, first * PACK : last * PACK],
+            )
+
+        def copy(engine, dst, src):
+            if engine == "vector":
+                nc.vector.tensor_copy(out=dst, in_=src)
+            else:
+                nc.scalar.copy(out=dst, in_=src)
+
+        w_rows = sbuf.tile([P, PACK * D], BF16, name="w_rows")
+        w_mx = quantisable("w", D)
+        x_rows = [sbuf.tile([P, PACK * D], BF16, name="x_rows%d" % r) for r in range(2 * B)]
+        x_mx = [quantisable("x%d" % r, L) for r in range(2 * B)]
+        h_mx = [quantisable("h%d" % b, L) for b in range(B)]
+        out_rows = [sbuf.tile([P, PACK * L], F32, name="out_rows%d" % b) for b in range(B)]
+        identity = sbuf.tile([P, P], F32, name="identity")
+
+        nc.sync.dma_start(out=w_rows[:], in_=bi_linear_w.rearrange("(p k) c -> p (k c)", k=PACK))
+        for b in range(B):
+            nc.sync.dma_start(out=x_rows[2 * b][:], in_=x1[b].rearrange("(q i) d -> q (i d)", i=4))
+            nc.sync.dma_start(
+                out=x_rows[2 * b + 1][:].rearrange("p (h r) -> p h r", h=2),
+                in_=x2[b].rearrange("(h q i) d -> q h (i d)", h=2, i=2),
+            )
+        make_identity(nc, identity[:])
+
+        banks = {}
+
+        def regroup_w(t, engine):
+            columns = w_rows[:].rearrange("p (k m t) -> p k m t", k=PACK, t=PACK)[:, :, :, t]
+            copy(
+                engine,
+                w_mx[0][:, t * P * PACK : (t + 1) * P * PACK].rearrange("p (m k) -> p m k", k=PACK),
+                columns.rearrange("p k m -> p m k"),
+            )
+
+        def transpose_x(r):
+            pairs = x_rows[r][:].bitcast(F32)
+            for half in range(2):
+                bank = psum.tile([P, BANK], F32, tag="bank", name="x_bank")
+                for block in range(4):
+                    i, u = block // 2, block % 2
+                    position = pairs[:, half * BANK + i * 2 * P : half * BANK + (i + 1) * 2 * P]
+                    nc.tensor.transpose(bank[:, block * P : (block + 1) * P], position[:, u::2], identity[:])
+                banks[("x", r, half)] = bank
+
+        def regroup_x(r, half, engine):
+            bank = banks[("x", r, half)]
+            grouped = x_mx[r][0][:].bitcast(F32)[:, half * BANK : (half + 1) * BANK]
+            if r % 2 == 0:
+                copy(
+                    engine,
+                    grouped.rearrange("p (i q u) -> p i q u", i=2, u=2),
+                    bank[:].rearrange("p (i u q) -> p i q u", i=2, u=2),
+                )
+            else:
+                copy(
+                    engine,
+                    grouped.rearrange("p (q block) -> p q block", block=4),
+                    bank[:].rearrange("p (block q) -> p q block", block=4),
+                )
+
+        def quantise_x(r):
+            if r % 2 == 0:
+                quantise(x_mx[r], 0, L // 2)
+                quantise(x_mx[r], L // 2, L)
+            else:
+                quantise(x_mx[r], 0, L)
+
+        def tiles_of(j):
+            return [(j // 2, 2 * (j % 2)), (j // 2, 2 * (j % 2) + 1)]
+
+        def first_matmul(j):
+            for b, i in tiles_of(j):
+                bank = psum.tile([P, BANK], F32, tag="bank", name="h_bank")
+                for t in range(PACK):
+                    nc.tensor.matmul_mx(
+                        out=bank[:, t * P : (t + 1) * P],
+                        lhsT=w_mx[1][:, t * P : (t + 1) * P].bitcast(FP8X4),
+                        lhsT_scale=w_mx[2][:, t * P : (t + 1) * P],
+                        rhs=x_mx[2 * b][1][:, i * P : (i + 1) * P].bitcast(FP8X4),
+                        rhs_scale=x_mx[2 * b][2][:, i * P : (i + 1) * P],
+                        start=True,
+                        stop=True,
+                    )
+                banks[("h", b, i)] = bank
+
+        def round_h(tile, engine):
+            b, i = tile
+            copy(
+                engine,
+                h_mx[b][0][:, i * P * PACK : (i + 1) * P * PACK].rearrange("p (q t) -> p q t", t=PACK),
+                banks[("h", b, i)][:].rearrange("p (t q) -> p q t", t=PACK),
+            )
+
+        def quantise_h(tile):
+            b, i = tile
+            quantise(h_mx[b], i * P, (i + 1) * P)
+
+        def second_matmul(j):
+            for b, i in tiles_of(j):
+                bank = psum.tile([P, BANK], F32, tag="bank", name="sim_bank")
+                nc.tensor.matmul_mx(
+                    out=bank[:],
+                    lhsT=h_mx[b][1][:, i * P : (i + 1) * P].bitcast(FP8X4),
+                    lhsT_scale=h_mx[b][2][:, i * P : (i + 1) * P],
+                    rhs=x_mx[2 * b + 1][1][:].bitcast(FP8X4),
+                    rhs_scale=x_mx[2 * b + 1][2][:],
+                    start=True,
+                    stop=True,
+                )
+                banks[("sim", b, i)] = bank
+
+        def store_sim(tile, engine):
+            b, i = tile
+            copy(engine, out_rows[b][:, i * L : (i + 1) * L], banks[("sim", b, i)][:])
+            nc.sync.dma_start(
+                out=out[b].rearrange("(q i) m -> q (i m)", i=4)[:, i * L : (i + 1) * L],
+                in_=out_rows[b][:, i * L : (i + 1) * L],
+            )
+
+        for t in range(PACK):
+            regroup_w(t, "scalar" if t == PACK - 1 else "vector")
+        quantise(w_mx, 0, D // 2)
+        quantise(w_mx, D // 2, D)
+        transpose_x(0)
+        transpose_x(1)
+        regroup_x(0, 0, "scalar")
+        regroup_x(0, 1, "scalar")
+        quantise_x(0)
+        regroup_x(1, 0, "scalar")
+        regroup_x(1, 1, "vector")
+        quantise_x(1)
+        first_matmul(0)
+        transpose_x(2)
+
+        steps = 2 * B
+        for j in range(steps + 1):
+            last_step = j == steps - 1
+            if j < steps:
+                tile_a, tile_b = tiles_of(j)
+                round_h(tile_a, "scalar")
+                round_h(tile_b, "vector" if last_step else "scalar")
+                quantise_h(tile_a)
+                if last_step:
+                    quantise_h(tile_b)
+            if j > 0:
+                ready_a, ready_b = tiles_of(j - 1)
+                store_sim(ready_a, "scalar")
+                store_sim(ready_b, "vector")
+            if j < steps - 1:
+                quantise_h(tile_b)
+            if j + 2 < 2 * B:
+                regroup_x(j + 2, 0, "scalar")
+                regroup_x(j + 2, 1, "vector")
+                quantise_x(j + 2)
+            if j + 1 < steps:
+                first_matmul(j + 1)
+            if j < steps:
+                second_matmul(j)
+            if j + 3 < 2 * B:
+                transpose_x(j + 3)

@@ -52,6 +52,7 @@ def tile_coattentionandcombine_pa_kernel(tc, x1, bi_linear_w, x2, out):
         h_mx = [quantisable("h%d" % b, L) for b in range(B)]
         out_rows = [sbuf.tile([P, PACK * L], F32, name="out_rows%d" % b) for b in range(B)]
         identity = sbuf.tile([P, P], F32, name="identity")
+        zeros = sbuf.tile([P, BANK], BF16, name="zeros")
 
         nc.sync.dma_start(out=w_rows[:], in_=bi_linear_w.rearrange("(p k) c -> p (k c)", k=PACK))
         for b in range(B):
@@ -60,9 +61,15 @@ def tile_coattentionandcombine_pa_kernel(tc, x1, bi_linear_w, x2, out):
                 out=x_rows[2 * b + 1][:].rearrange("p (h r) -> p h r", h=2),
                 in_=x2[b].rearrange("(h q i) d -> q h (i d)", h=2, i=2),
             )
+        nc.vector.memset(zeros[:], 0.0)
         make_identity(nc, identity[:])
 
         banks = {}
+
+        def warm_up(passes):
+            bank = psum.tile([P, BANK], F32, tag="bank", name="zero_bank")
+            for n in range(passes):
+                nc.tensor.matmul(out=bank[:], lhsT=zeros[:, :P], rhs=zeros[:], start=True, stop=True)
 
         def regroup_w(t, engine):
             columns = w_rows[:].rearrange("p (k m t) -> p k m t", k=PACK, t=PACK)[:, :, :, t]
@@ -157,6 +164,7 @@ def tile_coattentionandcombine_pa_kernel(tc, x1, bi_linear_w, x2, out):
                 in_=out_rows[b][:, i * L : (i + 1) * L],
             )
 
+        warm_up(8)
         for t in range(PACK):
             regroup_w(t, "scalar" if t == PACK - 1 else "vector")
         quantise(w_mx, 0, D // 2)

@@ -56,7 +56,12 @@ def tile_coattentionandcombine_pa_kernel(tc, x1, bi_linear_w, x2, out):
 
         nc.sync.dma_start(out=w_rows[:], in_=bi_linear_w.rearrange("(p k) c -> p (k c)", k=PACK))
         for b in range(B):
-            nc.sync.dma_start(out=x_rows[2 * b][:], in_=x1[b].rearrange("(q i) d -> q (i d)", i=4))
+            rows = x1[b].rearrange("(q i) d -> q (i d)", i=4)
+            pieces = 2 if b == 0 else 1
+            for piece in range(pieces):
+                size = PACK * D // pieces
+                part = slice(piece * size, (piece + 1) * size)
+                nc.sync.dma_start(out=x_rows[2 * b][:, part], in_=rows[:, part])
             nc.sync.dma_start(
                 out=x_rows[2 * b + 1][:].rearrange("p (h r) -> p h r", h=2),
                 in_=x2[b].rearrange("(h q i) d -> q h (i d)", h=2, i=2),
@@ -164,20 +169,21 @@ def tile_coattentionandcombine_pa_kernel(tc, x1, bi_linear_w, x2, out):
                 in_=out_rows[b][:, i * L : (i + 1) * L],
             )
 
-        warm_up(8)
+        warm_up(7)
         for t in range(PACK):
             regroup_w(t, "scalar" if t == PACK - 1 else "vector")
         quantise(w_mx, 0, D // 2)
         quantise(w_mx, D // 2, D)
         transpose_x(0)
-        transpose_x(1)
+        warm_up(2)
         regroup_x(0, 0, "scalar")
-        regroup_x(0, 1, "scalar")
+        regroup_x(0, 1, "vector")
         quantise_x(0)
+        transpose_x(1)
+        first_matmul(0)
         regroup_x(1, 0, "scalar")
         regroup_x(1, 1, "vector")
         quantise_x(1)
-        first_matmul(0)
         transpose_x(2)
 
         steps = 2 * B

@@ -14,6 +14,7 @@ PACK = 4
 B, L, D = 3, 512, 512
 BANK = 512
 N_BANKS = 8
+SORTED = {2: (3,), 5: (2, 3,)}
 FLOPS = 2 * 2 * B * L * D * D
 
 
@@ -50,6 +51,7 @@ def tile_coattentionandcombine_pa_kernel(tc, x1, bi_linear_w, x2, out):
         x_rows = [sbuf.tile([P, PACK * D], BF16, name="x_rows%d" % r) for r in range(2 * B)]
         x_mx = [quantisable("x%d" % r, L) for r in range(2 * B)]
         h_mx = [quantisable("h%d" % b, L) for b in range(B)]
+        x_pairs = {r: sbuf.tile([P, 2 * BANK], F32, name="x_pairs%d" % r) for r in SORTED}
         out_rows = [sbuf.tile([P, PACK * L], F32, name="out_rows%d" % b) for b in range(B)]
         identity = sbuf.tile([P, P], F32, name="identity")
         zeros = sbuf.tile([P, BANK], BF16, name="zeros")
@@ -66,10 +68,17 @@ def tile_coattentionandcombine_pa_kernel(tc, x1, bi_linear_w, x2, out):
                 out=x_rows[2 * b + 1][:].rearrange("p (h r) -> p h r", h=2),
                 in_=x2[b].rearrange("(h q i) d -> q h (i d)", h=2, i=2),
             )
-        nc.vector.memset(zeros[:], 0.0)
+        nc.vector.memset(zeros[:].bitcast(U32), 0)
         make_identity(nc, identity[:])
 
         banks = {}
+
+        def sort_pairs(r):
+            for i in SORTED.get(r, ()):
+                nc.vector.tensor_copy(
+                    out=x_pairs[r][:, i * 2 * P : (i + 1) * 2 * P].rearrange("p (u m) -> p u m", u=2),
+                    in_=x_rows[r][:].bitcast(F32)[:, i * 2 * P : (i + 1) * 2 * P].rearrange("p (m u) -> p u m", u=2),
+                )
 
         def warm_up(passes):
             bank = psum.tile([P, BANK], F32, tag="bank", name="zero_bank")
@@ -91,7 +100,10 @@ def tile_coattentionandcombine_pa_kernel(tc, x1, bi_linear_w, x2, out):
                 for block in range(4):
                     i, u = block // 2, block % 2
                     position = pairs[:, half * BANK + i * 2 * P : half * BANK + (i + 1) * 2 * P]
-                    nc.tensor.transpose(bank[:, block * P : (block + 1) * P], position[:, u::2], identity[:])
+                    block_in = position[:, u::2]
+                    if 2 * half + i in SORTED.get(r, ()):
+                        block_in = x_pairs[r][:, half * BANK + block * P : half * BANK + (block + 1) * P]
+                    nc.tensor.transpose(bank[:, block * P : (block + 1) * P], block_in, identity[:])
                 banks[("x", r, half)] = bank
 
         def regroup_x(r, half, engine):
@@ -169,13 +181,13 @@ def tile_coattentionandcombine_pa_kernel(tc, x1, bi_linear_w, x2, out):
                 in_=out_rows[b][:, i * L : (i + 1) * L],
             )
 
-        warm_up(7)
+        warm_up(5)
         for t in range(PACK):
             regroup_w(t, "scalar" if t == PACK - 1 else "vector")
         quantise(w_mx, 0, D // 2)
         quantise(w_mx, D // 2, D)
         transpose_x(0)
-        warm_up(2)
+        warm_up(1)
         regroup_x(0, 0, "scalar")
         regroup_x(0, 1, "vector")
         quantise_x(0)
@@ -183,6 +195,7 @@ def tile_coattentionandcombine_pa_kernel(tc, x1, bi_linear_w, x2, out):
         first_matmul(0)
         regroup_x(1, 0, "scalar")
         regroup_x(1, 1, "vector")
+        sort_pairs(2)
         quantise_x(1)
         transpose_x(2)
 
@@ -205,6 +218,7 @@ def tile_coattentionandcombine_pa_kernel(tc, x1, bi_linear_w, x2, out):
             if j + 2 < 2 * B:
                 regroup_x(j + 2, 0, "scalar")
                 regroup_x(j + 2, 1, "vector")
+                sort_pairs(j + 4)
                 quantise_x(j + 2)
             if j + 1 < steps:
                 first_matmul(j + 1)

from contextlib import ExitStack

import concourse.mybir as mybir
from concourse.masks import make_identity

F32 = mybir.dt.float32
BF16 = mybir.dt.bfloat16
U32 = mybir.dt.uint32
U8 = mybir.dt.uint8
FP8X4 = mybir.dt.float8_e4m3fn_x4

P = 128
PACK = 4
B, L, D = 3, 512, 512
BANK = 512
N_BANKS = 8
SORTED = {2: (3,), 5: (2, 3,)}
FLOPS = 2 * 2 * B * L * D * D


def tile_coattentionandcombine_pa_kernel(tc, x1, bi_linear_w, x2, out):
    nc = tc.nc
    with ExitStack() as ctx:
        sbuf = ctx.enter_context(tc.tile_pool(name="sbuf", bufs=1))
        psum = ctx.enter_context(tc.psum_pool(name="psum", bufs=N_BANKS))
        ctx.enter_context(tc.manual_schedule())

        def quantisable(name, columns):
            return (
                sbuf.tile([P, columns * PACK], BF16, name=name + "_grouped", align_bytes=64),
                sbuf.tile([P, columns], U32, name=name + "_words", align_bytes=64),
                sbuf.tile([P, columns], U8, name=name + "_scales", align_bytes=64),
            )

        def quantise(operand, first, last):
            grouped, words, scales = operand
            nc.vector.quantize_mx(
                out=words[:, first:last].bitcast(FP8X4),
                scales=scales[:, first:last],
                in_=grouped[:, first * PACK : last * PACK],
            )

        def copy(engine, dst, src):
            if engine == "vector":
                nc.vector.tensor_copy(out=dst, in_=src)
            else:
                nc.scalar.copy(out=dst, in_=src)

        w_rows = sbuf.tile([P, PACK * D], BF16, name="w_rows")
        w_mx = quantisable("w", D)
        x_rows = [sbuf.tile([P, PACK * D], BF16, name="x_rows%d" % r) for r in range(2 * B)]
        x_mx = [quantisable("x%d" % r, L) for r in range(2 * B)]
        h_mx = [quantisable("h%d" % b, L) for b in range(B)]
        x_pairs = {r: sbuf.tile([P, 2 * BANK], F32, name="x_pairs%d" % r) for r in SORTED}
        out_rows = [sbuf.tile([P, PACK * L], F32, name="out_rows%d" % b) for b in range(B)]
        identity = sbuf.tile([P, P], F32, name="identity")
        zeros = sbuf.tile([P, BANK], BF16, name="zeros")

        nc.sync.dma_start(out=w_rows[:], in_=bi_linear_w.rearrange("(p k) c -> p (k c)", k=PACK))
        for b in range(B):
            rows = x1[b].rearrange("(q i) d -> q (i d)", i=4)
            pieces = 2 if b == 0 else 1
            for piece in range(pieces):
                size = PACK * D // pieces
                part = slice(piece * size, (piece + 1) * size)
                nc.sync.dma_start(out=x_rows[2 * b][:, part], in_=rows[:, part])
            nc.sync.dma_start(
                out=x_rows[2 * b + 1][:].rearrange("p (h r) -> p h r", h=2),
                in_=x2[b].rearrange("(h q i) d -> q h (i d)", h=2, i=2),
            )
        nc.vector.memset(zeros[:].bitcast(U32), 0)
        make_identity(nc, identity[:])

        banks = {}

        def sort_pairs(r):
            for i in SORTED.get(r, ()):
                nc.vector.tensor_copy(
                    out=x_pairs[r][:, i * 2 * P : (i + 1) * 2 * P].rearrange("p (u m) -> p u m", u=2),
                    in_=x_rows[r][:].bitcast(F32)[:, i * 2 * P : (i + 1) * 2 * P].rearrange("p (m u) -> p u m", u=2),
                )

        def warm_up(passes):
            bank = psum.tile([P, BANK], F32, tag="bank", name="zero_bank")
            for n in range(passes):
                nc.tensor.matmul(out=bank[:], lhsT=zeros[:, :P], rhs=zeros[:], start=True, stop=True)

        def regroup_w(t, engine):
            columns = w_rows[:].rearrange("p (k m t) -> p k m t", k=PACK, t=PACK)[:, :, :, t]
            copy(
                engine,
                w_mx[0][:, t * P * PACK : (t + 1) * P * PACK].rearrange("p (m k) -> p m k", k=PACK),
                columns.rearrange("p k m -> p m k"),
            )

        def transpose_x(r):
            pairs = x_rows[r][:].bitcast(F32)
            for half in range(2):
                bank = psum.tile([P, BANK], F32, tag="bank", name="x_bank")
                for block in range(4):
                    i, u = block // 2, block % 2
                    position = pairs[:, half * BANK + i * 2 * P : half * BANK + (i + 1) * 2 * P]
                    block_in = position[:, u::2]
                    if 2 * half + i in SORTED.get(r, ()):
                        block_in = x_pairs[r][:, half * BANK + block * P : half * BANK + (block + 1) * P]
                    nc.tensor.transpose(bank[:, block * P : (block + 1) * P], block_in, identity[:])
                banks[("x", r, half)] = bank

        def regroup_x(r, half, engine):
            bank = banks[("x", r, half)]
            grouped = x_mx[r][0][:].bitcast(F32)[:, half * BANK : (half + 1) * BANK]
            if r % 2 == 0:
                copy(
                    engine,
                    grouped.rearrange("p (i q u) -> p i q u", i=2, u=2),
                    bank[:].rearrange("p (i u q) -> p i q u", i=2, u=2),
                )
            else:
                copy(
                    engine,
                    grouped.rearrange("p (q block) -> p q block", block=4),
                    bank[:].rearrange("p (block q) -> p q block", block=4),
                )

        def quantise_x(r):
            if r % 2 == 0:
                quantise(x_mx[r], 0, L // 2)
                quantise(x_mx[r], L // 2, L)
            else:
                quantise(x_mx[r], 0, L)

        def tiles_of(j):
            return [(j // 2, 2 * (j % 2)), (j // 2, 2 * (j % 2) + 1)]

        def first_matmul(j):
            for b, i in tiles_of(j):
                bank = psum.tile([P, BANK], F32, tag="bank", name="h_bank")
                for t in range(PACK):
                    nc.tensor.matmul_mx(
                        out=bank[:, t * P : (t + 1) * P],
                        lhsT=w_mx[1][:, t * P : (t + 1) * P].bitcast(FP8X4),
                        lhsT_scale=w_mx[2][:, t * P : (t + 1) * P],
                        rhs=x_mx[2 * b][1][:, i * P : (i + 1) * P].bitcast(FP8X4),
                        rhs_scale=x_mx[2 * b][2][:, i * P : (i + 1) * P],
                        start=True,
                        stop=True,
                    )
                banks[("h", b, i)] = bank

        def round_h(tile, engine):
            b, i = tile
            copy(
                engine,
                h_mx[b][0][:, i * P * PACK : (i + 1) * P * PACK].rearrange("p (q t) -> p q t", t=PACK),
                banks[("h", b, i)][:].rearrange("p (t q) -> p q t", t=PACK),
            )

        def quantise_h(tile):
            b, i = tile
            quantise(h_mx[b], i * P, (i + 1) * P)

        def second_matmul(j):
            for b, i in tiles_of(j):
                bank = psum.tile([P, BANK], F32, tag="bank", name="sim_bank")
                nc.tensor.matmul_mx(
                    out=bank[:],
                    lhsT=h_mx[b][1][:, i * P : (i + 1) * P].bitcast(FP8X4),
                    lhsT_scale=h_mx[b][2][:, i * P : (i + 1) * P],
                    rhs=x_mx[2 * b + 1][1][:].bitcast(FP8X4),
                    rhs_scale=x_mx[2 * b + 1][2][:],
                    start=True,
                    stop=True,
                )
                banks[("sim", b, i)] = bank

        def store_sim(tile, engine):
            b, i = tile
            copy(engine, out_rows[b][:, i * L : (i + 1) * L], banks[("sim", b, i)][:])
            nc.sync.dma_start(
                out=out[b].rearrange("(q i) m -> q (i m)", i=4)[:, i * L : (i + 1) * L],
                in_=out_rows[b][:, i * L : (i + 1) * L],
            )

        warm_up(5)
        for t in range(PACK):
            regroup_w(t, "scalar" if t == PACK - 1 else "vector")
        quantise(w_mx, 0, D // 2)
        quantise(w_mx, D // 2, D)
        transpose_x(0)
        warm_up(1)
        regroup_x(0, 0, "scalar")
        regroup_x(0, 1, "vector")
        quantise_x(0)
        transpose_x(1)
        first_matmul(0)
        regroup_x(1, 0, "scalar")
        regroup_x(1, 1, "vector")
        sort_pairs(2)
        quantise_x(1)
        transpose_x(2)

        steps = 2 * B
        for j in range(steps + 1):
            last_step = j == steps - 1
            if j < steps:
                tile_a, tile_b = tiles_of(j)
                round_h(tile_a, "scalar")
                round_h(tile_b, "vector" if last_step else "scalar")
                quantise_h(tile_a)
                if last_step:
                    quantise_h(tile_b)
            if j > 0:
                ready_a, ready_b = tiles_of(j - 1)
                store_sim(ready_a, "scalar")
                store_sim(ready_b, "vector")
            if j < steps - 1:
                quantise_h(tile_b)
            if j + 2 < 2 * B:
                regroup_x(j + 2, 0, "scalar")
                regroup_x(j + 2, 1, "vector")
                sort_pairs(j + 4)
                quantise_x(j + 2)
            if j + 1 < steps:
                first_matmul(j + 1)
            if j < steps:
                second_matmul(j)
            if j + 3 < 2 * B:
                transpose_x(j + 3)
